import numpy as np
import ml_dtypes


def mxq(x, axis, fmt="e4m3"):
    dtype, down = {"e4m3": (ml_dtypes.float8_e4m3fn, 7), "e5m2": (ml_dtypes.float8_e5m2, 14)}[fmt]
    v = np.moveaxis(np.asarray(x, np.float32).astype(ml_dtypes.bfloat16).astype(np.float64), axis, -1)
    blocks = v.reshape(v.shape[:-1] + (-1, 32))
    amax = np.abs(blocks).max(-1, keepdims=True)
    byte = np.maximum(np.where(amax > 0, np.frexp(amax)[1] - 1 + 127, 0) - down, 1)
    scale = np.exp2(byte - 127.0)
    codes = (blocks / scale).astype(np.float32).astype(dtype).astype(np.float64)
    return np.moveaxis((codes * scale).reshape(v.shape), -1, axis)


WIDE = False


def mx_kscale(k):
    if not WIDE:
        return np.ones(k)
    levels = np.array([10, -10, 5, -5, 0])
    a = np.random.permutation(np.resize(levels, k // 512 * 4)).reshape(k // 512, 4)
    idx = np.arange(k)
    return np.exp2(a[idx // 512, idx % 128 // 32])


BF16 = ml_dtypes.bfloat16


def bf(x):
    return np.asarray(x, np.float32).astype(BF16)


def f64(x):
    return np.asarray(x).astype(np.float64)


E2M1 = np.array([0.0, 0.5, 1.0, 1.5, 2.0, 3.0, 4.0, 6.0, -0.0, -0.5, -1.0, -1.5, -2.0, -3.0, -4.0, -6.0])


def pack_weight(w, fmt):
    k, n = w.shape
    w = f64(bf(w)).reshape(k // 32, 32, n)
    amax = np.abs(w).max(1)
    if fmt == "e4m3":
        byte = np.frexp(amax)[1] - 1 + 127 - 7
    else:
        mant, ex = np.frexp(amax / 6.0)
        byte = np.where(mant > 0.5, ex, ex - 1) + 127
    byte = np.clip(np.where(amax > 0, byte, 1), 1, 254)
    scaled = (w * np.exp2(127.0 - byte)[:, None, :]).reshape(k, n).astype(np.float32)
    by_word = np.ascontiguousarray(scaled.reshape(k // 512, 128, 4, n).transpose(0, 1, 3, 2))
    if fmt == "e4m3":
        words = by_word.astype(ml_dtypes.float8_e4m3fn).view(np.uint8)
    else:
        c = by_word.astype(ml_dtypes.float4_e2m1fn).view(np.uint8) & 0xF
        words = c[..., 0::2] | (c[..., 1::2] << 4)
    return np.ascontiguousarray(words), np.ascontiguousarray(byte.astype(np.uint8).reshape(k // 512, 16, n))


def unpack_weight(words, scales, fmt):
    g, p, n, _ = words.shape
    if fmt == "e4m3":
        vals = np.ascontiguousarray(words).view(ml_dtypes.float8_e4m3fn).astype(np.float64)
    else:
        nib = np.empty((g, p, n, 4), np.uint8)
        nib[..., 0::2] = words & 0xF
        nib[..., 1::2] = words >> 4
        vals = E2M1[nib]
    vals = vals * np.repeat(np.exp2(scales.astype(np.float64) - 127.0), 8, axis=1)[..., None]
    return vals.transpose(0, 1, 3, 2).reshape(g * 512, n)


N, CI, CO, V, T = 1, 16384, 1024, 128, 1


def normalize_adjacency(adj):
    G = adj + np.eye(adj.shape[0])
    return G / G.sum(axis=1, keepdims=True)


def setup_inputs():
    s = mx_kscale(CI)
    adj = 0.1 * np.random.uniform(size=(V, V))
    i = np.arange(V - 1)
    adj[i, i + 1] += 1.0
    adj[i + 1, i] += 1.0
    x = bf(np.random.standard_normal((N, CI, V, T)) * s[None, :, None, None])
    A = bf(normalize_adjacency(adj))
    w = np.random.standard_normal((CO, CI)) * 4.0 / np.sqrt(CI) / s[None, :]
    W_words, W_scales = pack_weight(np.ascontiguousarray(w.T), "e4m3")
    b = bf(np.random.standard_normal(CO) * 0.5)
    return {"x": x,
            "A": A,
            "W_words": W_words,
            "W_scales": W_scales,
            "b": b}


def reference(x, A, W_words, W_scales, b):
    agg = (f64(x).transpose(0, 1, 3, 2) @ f64(A)).transpose(0, 1, 3, 2)
    aq = mxq(agg, 1, "e4m3")
    out = (unpack_weight(W_words, W_scales, "e4m3").T @ aq.reshape(N, CI, V * T)).reshape(N, CO, V, T)
    return out + f64(b)[None, :, None, None]

@@ -1,0 +1,156 @@
+from contextlib import ExitStack
+
+import concourse.mybir as mybir
+from concourse.masks import make_identity
+
+BF16 = mybir.dt.bfloat16
+F32 = mybir.dt.float32
+I32 = mybir.dt.int32
+U32 = mybir.dt.uint32
+U8 = mybir.dt.uint8
+FP8X4 = mybir.dt.float8_e4m3fn_x4
+
+P = 128
+PACK = 4
+K_PASS = P * PACK
+
+CI = 16384
+CO = 1024
+V = 128
+PASSES = CI // K_PASS
+CO_TILES = CO // P
+
+PLANES_PER_SLAB = 4
+SLABS = PASSES // PLANES_PER_SLAB
+QUADRANT = 32
+LIVE_ROWS = 4
+
+QUANT_PASSES = 4
+X_CHUNK = 4
+W_CHUNK = 2
+LAG = 2
+
+FLOPS = 2 * CI * V * V + 2 * CI * CO * V
+
+
+def tile_graphconv_k_kernel(tc, x, A, W_words, W_scales, b, out):
+    nc = tc.nc
+    with ExitStack() as ctx:
+        ctx.enter_context(tc.manual_schedule())
+        keep = ctx.enter_context(tc.tile_pool(name="keep", bufs=1))
+        stage = ctx.enter_context(tc.tile_pool(name="stage", bufs=4))
+
+        identity = keep.tile([P, P], BF16)
+        a_sb = keep.tile([P, V], BF16)
+        x_sb = keep.tile([P, PASSES, PACK * V], BF16)
+        w_words = keep.tile([P, PASSES, CO], U32, align_bytes=64)
+        w_planes = keep.tile([P, SLABS, CO], U8, align_bytes=64)
+        agg_words = keep.tile([P, PASSES, V], U32, align_bytes=64)
+        agg_planes = keep.tile([P, PASSES, V], U8, align_bytes=64)
+        b_rows = keep.tile([P, P], BF16)
+        b_cols = keep.tile([P, CO_TILES], F32)
+        out_sb = keep.tile([P, CO_TILES, V], F32)
+
+        make_identity(nc, identity[:])
+        nc.vector.memset(w_planes[:].bitcast(I32), 0)
+        nc.vector.memset(b_rows[:], 0.0)
+
+        nc.sync.dma_start(out=a_sb[:], in_=A)
+        x_view = x[0].rearrange("(g p t) v s -> p g (t v s)", p=P, t=PACK)
+        for g in range(0, PASSES, X_CHUNK):
+            nc.sync.dma_start(out=x_sb[:, g : g + X_CHUNK, :], in_=x_view[:, g : g + X_CHUNK, :])
+        nc.sync.dma_start(out=b_rows[0:CO_TILES, :], in_=b.rearrange("(j o) -> j o", o=P))
+        for g in range(0, PASSES, W_CHUNK):
+            nc.sync.dma_start(
+                out=w_words[:, g : g + W_CHUNK, :].bitcast(I32),
+                in_=W_words[g : g + W_CHUNK].rearrange("g p o t -> p g (o t)").bitcast(I32),
+            )
+        scale_view = W_scales.rearrange("(s j) (q r) o -> j r q s o", j=PLANES_PER_SLAB, r=LIVE_ROWS)
+        for j in range(PLANES_PER_SLAB):
+            for r in range(LIVE_ROWS):
+                nc.gpsimd.dma_start(
+                    out=w_planes[LIVE_ROWS * j + r : P : QUADRANT, :, :].bitcast(F32),
+                    in_=scale_view[j, r].bitcast(F32),
+                )
+
+        xT_of = {}
+        grouped_of = {}
+
+        def transpose_pass(psum_t, g):
+            xT_ps = psum_t.tile([P, PACK, P], BF16, name="xT_ps")
+            for t in range(PACK):
+                nc.tensor.transpose(xT_ps[:, t, :], x_sb[:, g, t * V : (t + 1) * V], identity[:])
+            xT_sb = stage.tile([P, PACK, P], BF16, name="xT_sb")
+            nc.vector.tensor_copy(out=xT_sb[:], in_=xT_ps[:])
+            xT_of[g] = xT_sb
+
+        def aggregate_pass(psum_a, g):
+            agg_ps = psum_a.tile([P, PACK, V], F32, name="agg_ps")
+            for t in range(PACK):
+                nc.tensor.matmul(agg_ps[:, t, :], lhsT=xT_of[g][:, t, :], rhs=a_sb[:], start=True, stop=True)
+            if g % QUANT_PASSES == 0:
+                grouped_of[g // QUANT_PASSES] = stage.tile(
+                    [P, QUANT_PASSES, V, PACK], BF16, name="grouped", align_bytes=64
+                )
+            nc.scalar.copy(
+                out=grouped_of[g // QUANT_PASSES][:, g % QUANT_PASSES, :, :],
+                in_=agg_ps[:].rearrange("p t w -> p w t"),
+            )
+
+        def quantise_passes(n):
+            passes = slice(n * QUANT_PASSES, (n + 1) * QUANT_PASSES)
+            nc.vector.quantize_mx(
+                out=agg_words[:, passes, :].rearrange("p g w -> p (g w)").bitcast(FP8X4),
+                scales=agg_planes[:, passes, :].rearrange("p g w -> p (g w)"),
+                in_=grouped_of[n][:].rearrange("p g w t -> p (g w t)"),
+            )
+
+        with ExitStack() as part1:
+            psum_t = part1.enter_context(tc.psum_pool(name="psum_t", bufs=3))
+            psum_a = part1.enter_context(tc.psum_pool(name="psum_a", bufs=4))
+            psum_b = part1.enter_context(tc.psum_pool(name="psum_b", bufs=1))
+            for step in range(PASSES + LAG):
+                if step < PASSES:
+                    transpose_pass(psum_t, step)
+                g = step - LAG
+                if g >= 0:
+                    aggregate_pass(psum_a, g)
+                    if g > 0 and g % QUANT_PASSES == 0:
+                        quantise_passes(g // QUANT_PASSES - 1)
+            quantise_passes(PASSES // QUANT_PASSES - 1)
+
+            bT_ps = psum_b.tile([P, P], BF16)
+            nc.tensor.transpose(bT_ps[:], b_rows[:], identity[:])
+            nc.vector.tensor_copy(out=b_cols[:], in_=bT_ps[:, 0:CO_TILES])
+
+        out_view = out[0].rearrange("(j o) w s -> o j (w s)", o=P)
+        with tc.psum_pool(name="psum_o", bufs=1) as psum_o:
+            acc = [psum_o.tile([P, V], F32, name="acc%d" % j) for j in range(CO_TILES)]
+            for g in range(PASSES):
+                slab = g // PLANES_PER_SLAB
+                plane_start = LIVE_ROWS * (g % PLANES_PER_SLAB)
+                for j in range(CO_TILES):
+                    cols = slice(j * P, (j + 1) * P)
+                    nc.tensor.matmul_mx(
+                        out=acc[j][:],
+                        lhsT=w_words[:, g, cols].bitcast(FP8X4),
+                        lhsT_scale=w_planes[plane_start:P, slab, cols],
+                        rhs=agg_words[:, g, :].bitcast(FP8X4),
+                        rhs_scale=agg_planes[:, g, :],
+                        start=(g == 0),
+                        stop=(g == PASSES - 1),
+                    )
+            for j in range(CO_TILES):
+                if j % 2 == 0:
+                    nc.scalar.activation(
+                        out=out_sb[:, j, :],
+                        in_=acc[j][:],
+                        func=mybir.ActivationFunctionType.Identity,
+                        bias=b_cols[:, j : j + 1],
+                        scale=1.0,
+                    )
+                else:
+                    nc.vector.tensor_scalar_add(out_sb[:, j, :], acc[j][:], b_cols[:, j : j + 1])
+            half = CO_TILES // 2
+            nc.sync.dma_start(out=out_view[:, 0:half, :], in_=out_sb[:, 0:half, :])
+            nc.sync.dma_start(out=out_view[:, half:CO_TILES, :], in_=out_sb[:, half:CO_TILES, :])

@@ -60,18 +60,27 @@ def tile_graphconv_k_kernel(tc, x, A, W_words, W_scales, b, out):
         for g in range(0, PASSES, X_CHUNK):
             nc.sync.dma_start(out=x_sb[:, g : g + X_CHUNK, :], in_=x_view[:, g : g + X_CHUNK, :])
         nc.sync.dma_start(out=b_rows[0:CO_TILES, :], in_=b.rearrange("(j o) -> j o", o=P))
-        for g in range(0, PASSES, W_CHUNK):
-            nc.sync.dma_start(
-                out=w_words[:, g : g + W_CHUNK, :].bitcast(I32),
-                in_=W_words[g : g + W_CHUNK].rearrange("g p o t -> p g (o t)").bitcast(I32),
-            )
-        scale_view = W_scales.rearrange("(s j) (q r) o -> j r q s o", j=PLANES_PER_SLAB, r=LIVE_ROWS)
-        for j in range(PLANES_PER_SLAB):
-            for r in range(LIVE_ROWS):
-                nc.gpsimd.dma_start(
-                    out=w_planes[LIVE_ROWS * j + r : P : QUADRANT, :, :].bitcast(F32),
-                    in_=scale_view[j, r].bitcast(F32),
+
+        def load_slab_scales(slab):
+            passes = slice(slab * PLANES_PER_SLAB, (slab + 1) * PLANES_PER_SLAB)
+            for q in range(P // QUADRANT):
+                nc.sync.dma_start(
+                    out=w_planes[q * QUADRANT : q * QUADRANT + PLANES_PER_SLAB * LIVE_ROWS, slab, :].bitcast(I32),
+                    in_=W_scales[passes, q * LIVE_ROWS : (q + 1) * LIVE_ROWS, :].bitcast(I32),
                 )
+
+        def load_slab_words(slab):
+            for g in range(slab * PLANES_PER_SLAB, (slab + 1) * PLANES_PER_SLAB, W_CHUNK):
+                nc.sync.dma_start(
+                    out=w_words[:, g : g + W_CHUNK, :].bitcast(I32),
+                    in_=W_words[g : g + W_CHUNK].rearrange("g p o t -> p g (o t)").bitcast(I32),
+                )
+
+        load_slab_scales(0)
+        for slab in range(SLABS):
+            if slab + 1 < SLABS:
+                load_slab_scales(slab + 1)
+            load_slab_words(slab)
 
         xT_of = {}
         grouped_of = {}

@@ -64,9 +64,9 @@ def tile_graphconv_k_kernel(tc, x, A, W_words, W_scales, b, out):
         def load_slab_scales(slab):
             passes = slice(slab * PLANES_PER_SLAB, (slab + 1) * PLANES_PER_SLAB)
             for q in range(P // QUADRANT):
-                nc.sync.dma_start(
-                    out=w_planes[q * QUADRANT : q * QUADRANT + PLANES_PER_SLAB * LIVE_ROWS, slab, :].bitcast(I32),
-                    in_=W_scales[passes, q * LIVE_ROWS : (q + 1) * LIVE_ROWS, :].bitcast(I32),
+                nc.gpsimd.dma_start(
+                    out=w_planes[q * QUADRANT : q * QUADRANT + PLANES_PER_SLAB * LIVE_ROWS, slab, :].bitcast(F32),
+                    in_=W_scales[passes, q * LIVE_ROWS : (q + 1) * LIVE_ROWS, :].bitcast(F32),
                 )
 
         def load_slab_words(slab):
@@ -76,10 +76,8 @@ def tile_graphconv_k_kernel(tc, x, A, W_words, W_scales, b, out):
                     in_=W_words[g : g + W_CHUNK].rearrange("g p o t -> p g (o t)").bitcast(I32),
                 )
 
-        load_slab_scales(0)
         for slab in range(SLABS):
-            if slab + 1 < SLABS:
-                load_slab_scales(slab + 1)
+            load_slab_scales(slab)
             load_slab_words(slab)
 
         xT_of = {}

@@ -25,10 +25,10 @@ SLABS = PASSES // PLANES_PER_SLAB
 QUADRANT = 32
 LIVE_ROWS = 4
 
-QUANT_PASSES = 4
-X_CHUNK = 4
+SLAB_ROWS = PLANES_PER_SLAB * PACK
+SLAB_PARTS = P // PLANES_PER_SLAB
+T_HALF = PACK // 2
 W_CHUNK = 2
-LAG = 2
 
 FLOPS = 2 * CI * V * V + 2 * CI * CO * V
 
@@ -42,7 +42,7 @@ def tile_graphconv_k_kernel(tc, x, A, W_words, W_scales, b, out):
 
         identity = keep.tile([P, P], BF16)
         a_sb = keep.tile([P, V], BF16)
-        x_sb = keep.tile([P, PASSES, PACK * V], BF16)
+        x_sb = keep.tile([P, SLABS, SLAB_ROWS * V], BF16)
         w_words = keep.tile([P, PASSES, CO], U32, align_bytes=64)
         w_planes = keep.tile([P, SLABS, CO], U8, align_bytes=64)
         agg_words = keep.tile([P, PASSES, V], U32, align_bytes=64)
@@ -56,9 +56,9 @@ def tile_graphconv_k_kernel(tc, x, A, W_words, W_scales, b, out):
         nc.vector.memset(b_rows[:], 0.0)
 
         nc.sync.dma_start(out=a_sb[:], in_=A)
-        x_view = x[0].rearrange("(g p t) v s -> p g (t v s)", p=P, t=PACK)
-        for g in range(0, PASSES, X_CHUNK):
-            nc.sync.dma_start(out=x_sb[:, g : g + X_CHUNK, :], in_=x_view[:, g : g + X_CHUNK, :])
+        x_view = x[0].rearrange("(s i r) v one -> i s (r v one)", i=P, r=SLAB_ROWS)
+        for slab in range(SLABS):
+            nc.sync.dma_start(out=x_sb[:, slab, :], in_=x_view[:, slab, :])
         nc.sync.dma_start(out=b_rows[0:CO_TILES, :], in_=b.rearrange("(j o) -> j o", o=P))
 
         def load_slab_scales(slab):
@@ -83,50 +83,50 @@ def tile_graphconv_k_kernel(tc, x, A, W_words, W_scales, b, out):
         xT_of = {}
         grouped_of = {}
 
-        def transpose_pass(psum_t, g):
-            xT_ps = psum_t.tile([P, PACK, P], BF16, name="xT_ps")
-            for t in range(PACK):
-                nc.tensor.transpose(xT_ps[:, t, :], x_sb[:, g, t * V : (t + 1) * V], identity[:])
-            xT_sb = stage.tile([P, PACK, P], BF16, name="xT_sb")
-            nc.vector.tensor_copy(out=xT_sb[:], in_=xT_ps[:])
-            xT_of[g] = xT_sb
+        def transpose_slab(psum_t, slab):
+            for half in range(PACK // T_HALF):
+                xT_ps = psum_t.tile([P, T_HALF, PLANES_PER_SLAB, P], BF16, name="xT_ps")
+                for t in range(T_HALF):
+                    for h in range(PLANES_PER_SLAB):
+                        row = PACK * h + T_HALF * half + t
+                        nc.tensor.transpose(xT_ps[:, t, h, :], x_sb[:, slab, row * V : (row + 1) * V], identity[:])
+                xT_sb = stage.tile([P, T_HALF, P, PLANES_PER_SLAB], BF16, name="xT_sb")
+                nc.vector.tensor_copy(out=xT_sb[:], in_=xT_ps[:].rearrange("v t h i -> v t i h"))
+                xT_of[slab, half] = xT_sb
 
-        def aggregate_pass(psum_a, g):
-            agg_ps = psum_a.tile([P, PACK, V], F32, name="agg_ps")
-            for t in range(PACK):
-                nc.tensor.matmul(agg_ps[:, t, :], lhsT=xT_of[g][:, t, :], rhs=a_sb[:], start=True, stop=True)
-            if g % QUANT_PASSES == 0:
-                grouped_of[g // QUANT_PASSES] = stage.tile(
-                    [P, QUANT_PASSES, V, PACK], BF16, name="grouped", align_bytes=64
-                )
-            nc.scalar.copy(
-                out=grouped_of[g // QUANT_PASSES][:, g % QUANT_PASSES, :, :],
-                in_=agg_ps[:].rearrange("p t w -> p w t"),
-            )
+        def aggregate_slab(psum_a, slab):
+            grouped = stage.tile([P, PLANES_PER_SLAB, V, PACK], BF16, name="grouped", align_bytes=64)
+            for j in range(PLANES_PER_SLAB):
+                agg_ps = psum_a.tile([P, PACK, V], F32, name="agg_ps")
+                for t in range(PACK):
+                    xT_pass = xT_of[slab, t // T_HALF][:, t % T_HALF, j * SLAB_PARTS : (j + 1) * SLAB_PARTS, :]
+                    nc.tensor.matmul(
+                        agg_ps[:, t, :], lhsT=xT_pass.rearrange("v i h -> v (i h)"), rhs=a_sb[:], start=True, stop=True
+                    )
+                nc.scalar.copy(out=grouped[:, j, :, :], in_=agg_ps[:].rearrange("p t w -> p w t"))
+            grouped_of[slab] = grouped
 
-        def quantise_passes(n):
-            passes = slice(n * QUANT_PASSES, (n + 1) * QUANT_PASSES)
+        def quantise_slab(slab):
+            passes = slice(slab * PLANES_PER_SLAB, (slab + 1) * PLANES_PER_SLAB)
             nc.vector.quantize_mx(
                 out=agg_words[:, passes, :].rearrange("p g w -> p (g w)").bitcast(FP8X4),
                 scales=agg_planes[:, passes, :].rearrange("p g w -> p (g w)"),
-                in_=grouped_of[n][:].rearrange("p g w t -> p (g w t)"),
+                in_=grouped_of[slab][:].rearrange("p g w t -> p (g w t)"),
             )
 
         with ExitStack() as part1:
-            psum_t = part1.enter_context(tc.psum_pool(name="psum_t", bufs=3))
+            psum_t = part1.enter_context(tc.psum_pool(name="psum_t", bufs=4))
             psum_a = part1.enter_context(tc.psum_pool(name="psum_a", bufs=4))
-            psum_b = part1.enter_context(tc.psum_pool(name="psum_b", bufs=1))
-            for step in range(PASSES + LAG):
-                if step < PASSES:
-                    transpose_pass(psum_t, step)
-                g = step - LAG
-                if g >= 0:
-                    aggregate_pass(psum_a, g)
-                    if g > 0 and g % QUANT_PASSES == 0:
-                        quantise_passes(g // QUANT_PASSES - 1)
-            quantise_passes(PASSES // QUANT_PASSES - 1)
+            transpose_slab(psum_t, 0)
+            for slab in range(SLABS):
+                if slab + 1 < SLABS:
+                    transpose_slab(psum_t, slab + 1)
+                if slab >= 1:
+                    quantise_slab(slab - 1)
+                aggregate_slab(psum_a, slab)
+            quantise_slab(SLABS - 1)
 
-            bT_ps = psum_b.tile([P, P], BF16)
+            bT_ps = psum_t.tile([P, P], BF16, tag="xT_ps")
             nc.tensor.transpose(bT_ps[:], b_rows[:], identity[:])
             nc.vector.tensor_copy(out=b_cols[:], in_=bT_ps[:, 0:CO_TILES])
 

@@ -29,6 +29,10 @@ SLAB_ROWS = PLANES_PER_SLAB * PACK
 SLAB_PARTS = P // PLANES_PER_SLAB
 T_HALF = PACK // 2
 W_CHUNK = 2
+HALVES = 2
+HALF_TILES = CO_TILES // HALVES
+HALF_COLS = CO // HALVES
+TAIL = PASSES - W_CHUNK
 
 FLOPS = 2 * CI * V * V + 2 * CI * CO * V
 
@@ -71,10 +75,14 @@ def tile_graphconv_k_kernel(tc, x, A, W_words, W_scales, b, out):
 
         def load_slab_words(slab):
             for g in range(slab * PLANES_PER_SLAB, (slab + 1) * PLANES_PER_SLAB, W_CHUNK):
-                nc.sync.dma_start(
-                    out=w_words[:, g : g + W_CHUNK, :].bitcast(I32),
-                    in_=W_words[g : g + W_CHUNK].rearrange("g p o t -> p g (o t)").bitcast(I32),
-                )
+                parts = HALVES if g == TAIL else 1
+                width = CO // parts
+                for part in range(parts):
+                    cols = slice(part * width, (part + 1) * width)
+                    nc.sync.dma_start(
+                        out=w_words[:, g : g + W_CHUNK, cols].bitcast(I32),
+                        in_=W_words[g : g + W_CHUNK, :, cols, :].rearrange("g p o t -> p g (o t)").bitcast(I32),
+                    )
 
         for slab in range(SLABS):
             load_slab_scales(slab)
@@ -133,10 +141,11 @@ def tile_graphconv_k_kernel(tc, x, A, W_words, W_scales, b, out):
         out_view = out[0].rearrange("(j o) w s -> o j (w s)", o=P)
         with tc.psum_pool(name="psum_o", bufs=1) as psum_o:
             acc = [psum_o.tile([P, V], F32, name="acc%d" % j) for j in range(CO_TILES)]
-            for g in range(PASSES):
+
+            def mx_pass(g, tiles):
                 slab = g // PLANES_PER_SLAB
                 plane_start = LIVE_ROWS * (g % PLANES_PER_SLAB)
-                for j in range(CO_TILES):
+                for j in tiles:
                     cols = slice(j * P, (j + 1) * P)
                     nc.tensor.matmul_mx(
                         out=acc[j][:],
@@ -147,17 +156,23 @@ def tile_graphconv_k_kernel(tc, x, A, W_words, W_scales, b, out):
                         start=(g == 0),
                         stop=(g == PASSES - 1),
                     )
-            for j in range(CO_TILES):
-                if j % 2 == 0:
-                    nc.scalar.activation(
-                        out=out_sb[:, j, :],
-                        in_=acc[j][:],
-                        func=mybir.ActivationFunctionType.Identity,
-                        bias=b_cols[:, j : j + 1],
-                        scale=1.0,
-                    )
-                else:
-                    nc.vector.tensor_scalar_add(out_sb[:, j, :], acc[j][:], b_cols[:, j : j + 1])
-            half = CO_TILES // 2
-            nc.sync.dma_start(out=out_view[:, 0:half, :], in_=out_sb[:, 0:half, :])
-            nc.sync.dma_start(out=out_view[:, half:CO_TILES, :], in_=out_sb[:, half:CO_TILES, :])
+
+            for g in range(TAIL):
+                mx_pass(g, range(CO_TILES))
+            for half in range(HALVES):
+                tiles = range(half * HALF_TILES, (half + 1) * HALF_TILES)
+                for g in range(TAIL, PASSES):
+                    mx_pass(g, tiles)
+                for j in tiles:
+                    if j % 2 == 0:
+                        nc.scalar.activation(
+                            out=out_sb[:, j, :],
+                            in_=acc[j][:],
+                            func=mybir.ActivationFunctionType.Identity,
+                            bias=b_cols[:, j : j + 1],
+                            scale=1.0,
+                        )
+                    else:
+                        nc.vector.tensor_scalar_add(out_sb[:, j, :], acc[j][:], b_cols[:, j : j + 1])
+                done = slice(half * HALF_TILES, (half + 1) * HALF_TILES)
+                nc.sync.dma_start(out=out_view[:, done, :], in_=out_sb[:, done, :])

@@ -29,6 +29,7 @@ SLAB_ROWS = PLANES_PER_SLAB * PACK
 SLAB_PARTS = P // PLANES_PER_SLAB
 T_HALF = PACK // 2
 W_CHUNK = 2
+BIAS_SLAB = 5
 HALVES = 2
 HALF_TILES = CO_TILES // HALVES
 HALF_COLS = CO // HALVES
@@ -42,7 +43,9 @@ def tile_graphconv_k_kernel(tc, x, A, W_words, W_scales, b, out):
     with ExitStack() as ctx:
         ctx.enter_context(tc.manual_schedule())
         keep = ctx.enter_context(tc.tile_pool(name="keep", bufs=1))
-        stage = ctx.enter_context(tc.tile_pool(name="stage", bufs=4))
+        stage = ctx.enter_context(tc.tile_pool(name="stage", bufs=6))
+        groups = ctx.enter_context(tc.tile_pool(name="groups", bufs=4))
+        psum = ctx.enter_context(tc.psum_pool(name="psum", bufs=1))
 
         identity = keep.tile([P, P], BF16)
         a_sb = keep.tile([P, V], BF16)
@@ -91,28 +94,30 @@ def tile_graphconv_k_kernel(tc, x, A, W_words, W_scales, b, out):
         xT_of = {}
         grouped_of = {}
 
-        def transpose_slab(psum_t, slab):
+        def transpose_slab(slab):
             for half in range(PACK // T_HALF):
-                xT_ps = psum_t.tile([P, T_HALF, PLANES_PER_SLAB, P], BF16, name="xT_ps")
+                bank = (slab % 2) * (PACK // T_HALF) + half
+                xT_ps = psum.tile([P, T_HALF, PLANES_PER_SLAB, P], BF16, name="xT_ps", tag="bank%d" % bank)
                 for t in range(T_HALF):
                     for h in range(PLANES_PER_SLAB):
                         row = PACK * h + T_HALF * half + t
                         nc.tensor.transpose(xT_ps[:, t, h, :], x_sb[:, slab, row * V : (row + 1) * V], identity[:])
                 xT_sb = stage.tile([P, T_HALF, P, PLANES_PER_SLAB], BF16, name="xT_sb")
-                nc.vector.tensor_copy(out=xT_sb[:], in_=xT_ps[:].rearrange("v t h i -> v t i h"))
+                copy = nc.scalar.copy if slab < 2 and half == 1 else nc.vector.tensor_copy
+                copy(out=xT_sb[:], in_=xT_ps[:].rearrange("v t h i -> v t i h"))
                 xT_of[slab, half] = xT_sb
 
-        def aggregate_slab(psum_a, slab):
-            grouped = stage.tile([P, PLANES_PER_SLAB, V, PACK], BF16, name="grouped", align_bytes=64)
-            for j in range(PLANES_PER_SLAB):
-                agg_ps = psum_a.tile([P, PACK, V], F32, name="agg_ps")
-                for t in range(PACK):
-                    xT_pass = xT_of[slab, t // T_HALF][:, t % T_HALF, j * SLAB_PARTS : (j + 1) * SLAB_PARTS, :]
-                    nc.tensor.matmul(
-                        agg_ps[:, t, :], lhsT=xT_pass.rearrange("v i h -> v (i h)"), rhs=a_sb[:], start=True, stop=True
-                    )
-                nc.scalar.copy(out=grouped[:, j, :, :], in_=agg_ps[:].rearrange("p t w -> p w t"))
-            grouped_of[slab] = grouped
+        def aggregate(slab, j):
+            if j == 0:
+                grouped = groups.tile([P, PLANES_PER_SLAB, V, PACK], BF16, name="grouped", align_bytes=64)
+                grouped_of[slab] = grouped
+            agg_ps = psum.tile([P, PACK, V], F32, name="agg_ps", tag="bank%d" % (PLANES_PER_SLAB + j))
+            for t in range(PACK):
+                xT_pass = xT_of[slab, t // T_HALF][:, t % T_HALF, j * SLAB_PARTS : (j + 1) * SLAB_PARTS, :]
+                nc.tensor.matmul(
+                    agg_ps[:, t, :], lhsT=xT_pass.rearrange("v i h -> v (i h)"), rhs=a_sb[:], start=True, stop=True
+                )
+            nc.scalar.copy(out=grouped_of[slab][:, j, :, :], in_=agg_ps[:].rearrange("p t w -> p w t"))
 
         def quantise_slab(slab):
             passes = slice(slab * PLANES_PER_SLAB, (slab + 1) * PLANES_PER_SLAB)
@@ -122,57 +127,67 @@ def tile_graphconv_k_kernel(tc, x, A, W_words, W_scales, b, out):
                 in_=grouped_of[slab][:].rearrange("p g w t -> p (g w t)"),
             )
 
-        with ExitStack() as part1:
-            psum_t = part1.enter_context(tc.psum_pool(name="psum_t", bufs=4))
-            psum_a = part1.enter_context(tc.psum_pool(name="psum_a", bufs=4))
-            transpose_slab(psum_t, 0)
-            for slab in range(SLABS):
-                if slab + 1 < SLABS:
-                    transpose_slab(psum_t, slab + 1)
-                if slab >= 1:
-                    quantise_slab(slab - 1)
-                aggregate_slab(psum_a, slab)
-            quantise_slab(SLABS - 1)
+        acc = []
 
-            bT_ps = psum_t.tile([P, P], BF16, tag="xT_ps")
-            nc.tensor.transpose(bT_ps[:], b_rows[:], identity[:])
-            nc.vector.tensor_copy(out=b_cols[:], in_=bT_ps[:, 0:CO_TILES])
+        def open_output_tiles(first):
+            for j in range(first, first + HALF_TILES):
+                acc_ps = psum.tile([P, V], F32, name="acc_ps", tag="bank%d" % j)
+                acc.append(acc_ps)
 
+        def mx_pass(g, tiles):
+            slab = g // PLANES_PER_SLAB
+            plane_start = LIVE_ROWS * (g % PLANES_PER_SLAB)
+            for j in tiles:
+                cols = slice(j * P, (j + 1) * P)
+                nc.tensor.matmul_mx(
+                    out=acc[j][:],
+                    lhsT=w_words[:, g, cols].bitcast(FP8X4),
+                    lhsT_scale=w_planes[plane_start:P, slab, cols],
+                    rhs=agg_words[:, g, :].bitcast(FP8X4),
+                    rhs_scale=agg_planes[:, g, :],
+                    start=(g == 0),
+                    stop=(g == PASSES - 1),
+                )
+
+        transpose_slab(0)
+        for slab in range(SLABS - 1):
+            transpose_slab(slab + 1)
+            if slab >= 1:
+                quantise_slab(slab - 1)
+            for j in range(PLANES_PER_SLAB):
+                aggregate(slab, j)
+            if slab == BIAS_SLAB:
+                bT_ps = psum.tile([P, P], BF16, name="bT_ps", tag="bank%d" % PLANES_PER_SLAB)
+                nc.tensor.transpose(bT_ps[:], b_rows[:], identity[:])
+                nc.vector.tensor_copy(out=b_cols[:], in_=bT_ps[:, 0:CO_TILES])
+
+        quantise_slab(SLABS - 2)
+        open_output_tiles(0)
+        for j in range(PLANES_PER_SLAB):
+            aggregate(SLABS - 1, j)
+            mx_pass(j, range(HALF_TILES))
+        quantise_slab(SLABS - 1)
+
+        open_output_tiles(HALF_TILES)
+        for g in range(PLANES_PER_SLAB):
+            mx_pass(g, range(HALF_TILES, CO_TILES))
+        for g in range(PLANES_PER_SLAB, TAIL):
+            mx_pass(g, range(CO_TILES))
         out_view = out[0].rearrange("(j o) w s -> o j (w s)", o=P)
-        with tc.psum_pool(name="psum_o", bufs=1) as psum_o:
-            acc = [psum_o.tile([P, V], F32, name="acc%d" % j) for j in range(CO_TILES)]
-
-            def mx_pass(g, tiles):
-                slab = g // PLANES_PER_SLAB
-                plane_start = LIVE_ROWS * (g % PLANES_PER_SLAB)
-                for j in tiles:
-                    cols = slice(j * P, (j + 1) * P)
-                    nc.tensor.matmul_mx(
-                        out=acc[j][:],
-                        lhsT=w_words[:, g, cols].bitcast(FP8X4),
-                        lhsT_scale=w_planes[plane_start:P, slab, cols],
-                        rhs=agg_words[:, g, :].bitcast(FP8X4),
-                        rhs_scale=agg_planes[:, g, :],
-                        start=(g == 0),
-                        stop=(g == PASSES - 1),
+        for half in range(HALVES):
+            tiles = range(half * HALF_TILES, (half + 1) * HALF_TILES)
+            for g in range(TAIL, PASSES):
+                mx_pass(g, tiles)
+            for j in tiles:
+                if j % 2 == 0:
+                    nc.scalar.activation(
+                        out=out_sb[:, j, :],
+                        in_=acc[j][:],
+                        func=mybir.ActivationFunctionType.Identity,
+                        bias=b_cols[:, j : j + 1],
+                        scale=1.0,
                     )
-
-            for g in range(TAIL):
-                mx_pass(g, range(CO_TILES))
-            for half in range(HALVES):
-                tiles = range(half * HALF_TILES, (half + 1) * HALF_TILES)
-                for g in range(TAIL, PASSES):
-                    mx_pass(g, tiles)
-                for j in tiles:
-                    if j % 2 == 0:
-                        nc.scalar.activation(
-                            out=out_sb[:, j, :],
-                            in_=acc[j][:],
-                            func=mybir.ActivationFunctionType.Identity,
-                            bias=b_cols[:, j : j + 1],
-                            scale=1.0,
-                        )
-                    else:
-                        nc.vector.tensor_scalar_add(out_sb[:, j, :], acc[j][:], b_cols[:, j : j + 1])
-                done = slice(half * HALF_TILES, (half + 1) * HALF_TILES)
-                nc.sync.dma_start(out=out_view[:, done, :], in_=out_sb[:, done, :])
+                else:
+                    nc.vector.tensor_scalar_add(out_sb[:, j, :], acc[j][:], b_cols[:, j : j + 1])
+            done = slice(half * HALF_TILES, (half + 1) * HALF_TILES)
+            nc.sync.dma_start(out=out_view[:, done, :], in_=out_sb[:, done, :])

@@ -30,9 +30,8 @@ SLAB_PARTS = P // PLANES_PER_SLAB
 T_HALF = PACK // 2
 W_CHUNK = 2
 BIAS_SLAB = 5
-HALVES = 2
-HALF_TILES = CO_TILES // HALVES
-HALF_COLS = CO // HALVES
+HALF_TILES = CO_TILES // 2
+PIECES = (range(0, 4), range(4, 6), range(6, 8))
 TAIL = PASSES - W_CHUNK
 
 FLOPS = 2 * CI * V * V + 2 * CI * CO * V
@@ -78,10 +77,8 @@ def tile_graphconv_k_kernel(tc, x, A, W_words, W_scales, b, out):
 
         def load_slab_words(slab):
             for g in range(slab * PLANES_PER_SLAB, (slab + 1) * PLANES_PER_SLAB, W_CHUNK):
-                parts = HALVES if g == TAIL else 1
-                width = CO // parts
-                for part in range(parts):
-                    cols = slice(part * width, (part + 1) * width)
+                for tiles in PIECES if g == TAIL else (range(CO_TILES),):
+                    cols = slice(tiles.start * P, tiles.stop * P)
                     nc.sync.dma_start(
                         out=w_words[:, g : g + W_CHUNK, cols].bitcast(I32),
                         in_=W_words[g : g + W_CHUNK, :, cols, :].rearrange("g p o t -> p g (o t)").bitcast(I32),
@@ -174,8 +171,7 @@ def tile_graphconv_k_kernel(tc, x, A, W_words, W_scales, b, out):
         for g in range(PLANES_PER_SLAB, TAIL):
             mx_pass(g, range(CO_TILES))
         out_view = out[0].rearrange("(j o) w s -> o j (w s)", o=P)
-        for half in range(HALVES):
-            tiles = range(half * HALF_TILES, (half + 1) * HALF_TILES)
+        for tiles in PIECES:
             for g in range(TAIL, PASSES):
                 mx_pass(g, tiles)
             for j in tiles:
@@ -189,5 +185,5 @@ def tile_graphconv_k_kernel(tc, x, A, W_words, W_scales, b, out):
                     )
                 else:
                     nc.vector.tensor_scalar_add(out_sb[:, j, :], acc[j][:], b_cols[:, j : j + 1])
-            done = slice(half * HALF_TILES, (half + 1) * HALF_TILES)
+            done = slice(tiles.start, tiles.stop)
             nc.sync.dma_start(out=out_view[:, done, :], in_=out_sb[:, done, :])

from contextlib import ExitStack

import concourse.mybir as mybir
from concourse.masks import make_identity

BF16 = mybir.dt.bfloat16
F32 = mybir.dt.float32
I32 = mybir.dt.int32
U32 = mybir.dt.uint32
U8 = mybir.dt.uint8
FP8X4 = mybir.dt.float8_e4m3fn_x4

P = 128
PACK = 4
K_PASS = P * PACK

CI = 16384
CO = 1024
V = 128
PASSES = CI // K_PASS
CO_TILES = CO // P

PLANES_PER_SLAB = 4
SLABS = PASSES // PLANES_PER_SLAB
QUADRANT = 32
LIVE_ROWS = 4

SLAB_ROWS = PLANES_PER_SLAB * PACK
SLAB_PARTS = P // PLANES_PER_SLAB
T_HALF = PACK // 2
W_CHUNK = 2
BIAS_SLAB = 5
HALF_TILES = CO_TILES // 2
PIECES = (range(0, 4), range(4, 6), range(6, 8))
TAIL = PASSES - W_CHUNK

FLOPS = 2 * CI * V * V + 2 * CI * CO * V


def tile_graphconv_k_kernel(tc, x, A, W_words, W_scales, b, out):
    nc = tc.nc
    with ExitStack() as ctx:
        ctx.enter_context(tc.manual_schedule())
        keep = ctx.enter_context(tc.tile_pool(name="keep", bufs=1))
        stage = ctx.enter_context(tc.tile_pool(name="stage", bufs=6))
        groups = ctx.enter_context(tc.tile_pool(name="groups", bufs=4))
        psum = ctx.enter_context(tc.psum_pool(name="psum", bufs=1))

        identity = keep.tile([P, P], BF16)
        a_sb = keep.tile([P, V], BF16)
        x_sb = keep.tile([P, SLABS, SLAB_ROWS * V], BF16)
        w_words = keep.tile([P, PASSES, CO], U32, align_bytes=64)
        w_planes = keep.tile([P, SLABS, CO], U8, align_bytes=64)
        agg_words = keep.tile([P, PASSES, V], U32, align_bytes=64)
        agg_planes = keep.tile([P, PASSES, V], U8, align_bytes=64)
        b_rows = keep.tile([P, P], BF16)
        b_cols = keep.tile([P, CO_TILES], F32)
        out_sb = keep.tile([P, CO_TILES, V], F32)

        make_identity(nc, identity[:])
        nc.vector.memset(w_planes[:].bitcast(I32), 0)
        nc.vector.memset(b_rows[:], 0.0)

        nc.sync.dma_start(out=a_sb[:], in_=A)
        x_view = x[0].rearrange("(s i r) v one -> i s (r v one)", i=P, r=SLAB_ROWS)
        for slab in range(SLABS):
            nc.sync.dma_start(out=x_sb[:, slab, :], in_=x_view[:, slab, :])
        nc.sync.dma_start(out=b_rows[0:CO_TILES, :], in_=b.rearrange("(j o) -> j o", o=P))

        def load_slab_scales(slab):
            passes = slice(slab * PLANES_PER_SLAB, (slab + 1) * PLANES_PER_SLAB)
            for q in range(P // QUADRANT):
                nc.gpsimd.dma_start(
                    out=w_planes[q * QUADRANT : q * QUADRANT + PLANES_PER_SLAB * LIVE_ROWS, slab, :].bitcast(F32),
                    in_=W_scales[passes, q * LIVE_ROWS : (q + 1) * LIVE_ROWS, :].bitcast(F32),
                )

        def load_slab_words(slab):
            for g in range(slab * PLANES_PER_SLAB, (slab + 1) * PLANES_PER_SLAB, W_CHUNK):
                for tiles in PIECES if g == TAIL else (range(CO_TILES),):
                    cols = slice(tiles.start * P, tiles.stop * P)
                    nc.sync.dma_start(
                        out=w_words[:, g : g + W_CHUNK, cols].bitcast(I32),
                        in_=W_words[g : g + W_CHUNK, :, cols, :].rearrange("g p o t -> p g (o t)").bitcast(I32),
                    )

        for slab in range(SLABS):
            load_slab_scales(slab)
            load_slab_words(slab)

        xT_of = {}
        grouped_of = {}

        def transpose_slab(slab):
            for half in range(PACK // T_HALF):
                bank = (slab % 2) * (PACK // T_HALF) + half
                xT_ps = psum.tile([P, T_HALF, PLANES_PER_SLAB, P], BF16, name="xT_ps", tag="bank%d" % bank)
                for t in range(T_HALF):
                    for h in range(PLANES_PER_SLAB):
                        row = PACK * h + T_HALF * half + t
                        nc.tensor.transpose(xT_ps[:, t, h, :], x_sb[:, slab, row * V : (row + 1) * V], identity[:])
                xT_sb = stage.tile([P, T_HALF, P, PLANES_PER_SLAB], BF16, name="xT_sb")
                copy = nc.scalar.copy if slab < 2 and half == 1 else nc.vector.tensor_copy
                copy(out=xT_sb[:], in_=xT_ps[:].rearrange("v t h i -> v t i h"))
                xT_of[slab, half] = xT_sb

        def aggregate(slab, j):
            if j == 0:
                grouped = groups.tile([P, PLANES_PER_SLAB, V, PACK], BF16, name="grouped", align_bytes=64)
                grouped_of[slab] = grouped
            agg_ps = psum.tile([P, PACK, V], F32, name="agg_ps", tag="bank%d" % (PLANES_PER_SLAB + j))
            for t in range(PACK):
                xT_pass = xT_of[slab, t // T_HALF][:, t % T_HALF, j * SLAB_PARTS : (j + 1) * SLAB_PARTS, :]
                nc.tensor.matmul(
                    agg_ps[:, t, :], lhsT=xT_pass.rearrange("v i h -> v (i h)"), rhs=a_sb[:], start=True, stop=True
                )
            nc.scalar.copy(out=grouped_of[slab][:, j, :, :], in_=agg_ps[:].rearrange("p t w -> p w t"))

        def quantise_slab(slab):
            passes = slice(slab * PLANES_PER_SLAB, (slab + 1) * PLANES_PER_SLAB)
            nc.vector.quantize_mx(
                out=agg_words[:, passes, :].rearrange("p g w -> p (g w)").bitcast(FP8X4),
                scales=agg_planes[:, passes, :].rearrange("p g w -> p (g w)"),
                in_=grouped_of[slab][:].rearrange("p g w t -> p (g w t)"),
            )

        acc = []

        def open_output_tiles(first):
            for j in range(first, first + HALF_TILES):
                acc_ps = psum.tile([P, V], F32, name="acc_ps", tag="bank%d" % j)
                acc.append(acc_ps)

        def mx_pass(g, tiles):
            slab = g // PLANES_PER_SLAB
            plane_start = LIVE_ROWS * (g % PLANES_PER_SLAB)
            for j in tiles:
                cols = slice(j * P, (j + 1) * P)
                nc.tensor.matmul_mx(
                    out=acc[j][:],
                    lhsT=w_words[:, g, cols].bitcast(FP8X4),
                    lhsT_scale=w_planes[plane_start:P, slab, cols],
                    rhs=agg_words[:, g, :].bitcast(FP8X4),
                    rhs_scale=agg_planes[:, g, :],
                    start=(g == 0),
                    stop=(g == PASSES - 1),
                )

        transpose_slab(0)
        for slab in range(SLABS - 1):
            transpose_slab(slab + 1)
            if slab >= 1:
                quantise_slab(slab - 1)
            for j in range(PLANES_PER_SLAB):
                aggregate(slab, j)
            if slab == BIAS_SLAB:
                bT_ps = psum.tile([P, P], BF16, name="bT_ps", tag="bank%d" % PLANES_PER_SLAB)
                nc.tensor.transpose(bT_ps[:], b_rows[:], identity[:])
                nc.vector.tensor_copy(out=b_cols[:], in_=bT_ps[:, 0:CO_TILES])

        quantise_slab(SLABS - 2)
        open_output_tiles(0)
        for j in range(PLANES_PER_SLAB):
            aggregate(SLABS - 1, j)
            mx_pass(j, range(HALF_TILES))
        quantise_slab(SLABS - 1)

        open_output_tiles(HALF_TILES)
        for g in range(PLANES_PER_SLAB):
            mx_pass(g, range(HALF_TILES, CO_TILES))
        for g in range(PLANES_PER_SLAB, TAIL):
            mx_pass(g, range(CO_TILES))
        out_view = out[0].rearrange("(j o) w s -> o j (w s)", o=P)
        for tiles in PIECES:
            for g in range(TAIL, PASSES):
                mx_pass(g, tiles)
            for j in tiles:
                if j % 2 == 0:
                    nc.scalar.activation(
                        out=out_sb[:, j, :],
                        in_=acc[j][:],
                        func=mybir.ActivationFunctionType.Identity,
                        bias=b_cols[:, j : j + 1],
                        scale=1.0,
                    )
                else:
                    nc.vector.tensor_scalar_add(out_sb[:, j, :], acc[j][:], b_cols[:, j : j + 1])
            done = slice(tiles.start, tiles.stop)
            nc.sync.dma_start(out=out_view[:, done, :], in_=out_sb[:, done, :])
